import numpy as np
import ml_dtypes


def mxq(x, axis, fmt="e4m3"):
    dtype, down = {"e4m3": (ml_dtypes.float8_e4m3fn, 7), "e5m2": (ml_dtypes.float8_e5m2, 14)}[fmt]
    v = np.moveaxis(np.asarray(x, np.float32).astype(ml_dtypes.bfloat16).astype(np.float64), axis, -1)
    blocks = v.reshape(v.shape[:-1] + (-1, 32))
    amax = np.abs(blocks).max(-1, keepdims=True)
    byte = np.maximum(np.where(amax > 0, np.frexp(amax)[1] - 1 + 127, 0) - down, 1)
    scale = np.exp2(byte - 127.0)
    codes = (blocks / scale).astype(np.float32).astype(dtype).astype(np.float64)
    return np.moveaxis((codes * scale).reshape(v.shape), -1, axis)


WIDE = False


def mx_kscale(k):
    if not WIDE:
        return np.ones(k)
    levels = np.array([30, -30])
    if k % 512:
        return np.exp2(np.random.permutation(np.resize(levels, k // 32))).repeat(32)
    a = np.empty((k // 512, 16))
    for p in range(k // 512):
        a[p, :8] = np.random.permutation(np.resize(levels, 8))
        for g in range(8):
            far = levels[np.abs(levels - a[p, g]) >= 10]
            a[p, g + 8] = far[np.random.randint(len(far))]
    return np.exp2(a.ravel()).repeat(32)


BF16 = ml_dtypes.bfloat16


def bf(x):
    return np.asarray(x, np.float32).astype(BF16)


def f64(x):
    return np.asarray(x).astype(np.float64)


E2M1 = np.array([0.0, 0.5, 1.0, 1.5, 2.0, 3.0, 4.0, 6.0, -0.0, -0.5, -1.0, -1.5, -2.0, -3.0, -4.0, -6.0])


def pack_weight(w, fmt):
    k, n = w.shape
    w = f64(bf(w)).reshape(k // 32, 32, n)
    amax = np.abs(w).max(1)
    if fmt == "e4m3":
        byte = np.frexp(amax)[1] - 1 + 127 - 7
    else:
        mant, ex = np.frexp(amax / 6.0)
        byte = np.where(mant > 0.5, ex, ex - 1) + 127
    byte = np.clip(np.where(amax > 0, byte, 1), 1, 254)
    scaled = (w * np.exp2(127.0 - byte)[:, None, :]).reshape(k, n).astype(np.float32)
    by_word = np.ascontiguousarray(scaled.reshape(k // 512, 128, 4, n).transpose(0, 1, 3, 2))
    if fmt == "e4m3":
        words = by_word.astype(ml_dtypes.float8_e4m3fn).view(np.uint8)
    else:
        c = by_word.astype(ml_dtypes.float4_e2m1fn).view(np.uint8) & 0xF
        words = c[..., 0::2] | (c[..., 1::2] << 4)
    return np.ascontiguousarray(words), np.ascontiguousarray(byte.astype(np.uint8).reshape(k // 512, 16, n))


def unpack_weight(words, scales, fmt):
    g, p, n, _ = words.shape
    if fmt == "e4m3":
        vals = np.ascontiguousarray(words).view(ml_dtypes.float8_e4m3fn).astype(np.float64)
    else:
        nib = np.empty((g, p, n, 4), np.uint8)
        nib[..., 0::2] = words & 0xF
        nib[..., 1::2] = words >> 4
        vals = E2M1[nib]
    vals = vals * np.repeat(np.exp2(scales.astype(np.float64) - 127.0), 8, axis=1)[..., None]
    return vals.transpose(0, 1, 3, 2).reshape(g * 512, n)

def pack4(w):
    words, scales = pack_weight(w, "e2m1")
    return words.reshape(words.shape[0], 128, -1), scales


def unpack4(words, scales):
    return unpack_weight(words.reshape(words.shape[0], 128, -1, 2), scales, "e2m1")


B, T, D, H, KVH, HD = 2, 512, 2048, 16, 4, 128
HALF = HD // 2
EPS = 1e-6
ROPE_BASE = 10000.0


def zc_rmsnorm(x, scale):
    rms = np.sqrt(np.mean(x ** 2, axis=-1, keepdims=True) + EPS)
    return (1.0 + scale) * x / rms


def apply_rope(x, cos, sin):
    t = x.shape[2]
    c = cos[:t][None, None, :, :]
    s = sin[:t][None, None, :, :]
    x1, x2 = x[..., :HALF], x[..., HALF:]
    return np.concatenate([x1 * c - x2 * s, x2 * c + x1 * s], axis=-1)


def setup_inputs():
    s = mx_kscale(D)
    inv_freq = 1.0 / (ROPE_BASE ** (np.arange(0, HALF) / HALF))
    ang = np.arange(T)[:, None] * inv_freq[None, :]
    q_input = bf(np.random.standard_normal((B, T, D)) * s)
    words, scales = pack4(np.random.standard_normal((D, H * HD)) / np.sqrt(D) / s[:, None])
    return {"q_input": q_input,
            "Wq_words": words, "Wq_scales": scales,
            "q_scale": bf(np.random.standard_normal(HD) * 0.2),
            "cos": bf(np.cos(ang)), "sin": bf(np.sin(ang))}


def reference(q_input, Wq_words, Wq_scales, q_scale, cos, sin):
    b = q_input.shape[0]
    q = mxq(f64(q_input), 2, "e5m2") @ unpack4(Wq_words, Wq_scales)
    q = q.reshape(b, -1, H, HD).transpose(0, 2, 1, 3)
    q = zc_rmsnorm(q, f64(q_scale))
    return apply_rope(q, f64(cos), f64(sin))

@@ -1,0 +1,216 @@
+from contextlib import ExitStack
+
+import concourse.mybir as mybir
+from concourse.masks import make_identity
+
+B, T, D, H, HD = 2, 512, 2048, 16, 128
+HALF = HD // 2
+EPS = 1e-6
+FLOPS = 2 * B * T * D * H * HD
+
+F32 = mybir.dt.float32
+BF16 = mybir.dt.bfloat16
+I32 = mybir.dt.int32
+U32 = mybir.dt.uint32
+U8 = mybir.dt.uint8
+E5M2X4 = mybir.dt.float8_e5m2_x4
+E2M1X4 = mybir.dt.float4_e2m1fn_x4
+ALU = mybir.AluOpType
+ACT = mybir.ActivationFunctionType
+
+P = 128
+PASSES = D // 512
+CHUNK = 512
+CHUNKS = H * HD // CHUNK
+HEADS = CHUNK // HD
+PAIR = 2
+GROUP = P * PAIR
+GROUPS = B * T // GROUP
+TILES = GROUPS * PAIR
+BANKS = TILES * CHUNKS
+VECTOR_PAIRS = 2
+
+
+def tile_multiheadattention_pa_kernel(tc, q_input, Wq_words, Wq_scales, q_scale, cos, sin, out):
+    nc = tc.nc
+    x_rows = q_input.rearrange("b (u p j) k -> (b u) j p k", p=P, j=PAIR)
+    out_rows = out.rearrange("b h (u p j) d -> b u p h (j d)", p=P, j=PAIR)
+
+    with ExitStack() as ctx:
+        keep = ctx.enter_context(tc.tile_pool(name="keep", bufs=1))
+        work = ctx.enter_context(tc.tile_pool(name="work", bufs=2))
+        psum = ctx.enter_context(tc.psum_pool(name="psum", bufs=2))
+        ctx.enter_context(tc.manual_schedule())
+
+        ident = keep.tile([P, P], F32)
+        x_sb = [[keep.tile([P, D // 2], BF16, name=f"x{i}_{s}") for s in range(2)] for i in range(TILES)]
+        x_codes = [keep.tile([P, PASSES * P], U32, name=f"xc{i}", align_bytes=64) for i in range(TILES)]
+        x_scales = [keep.tile([P, PASSES * P], U8, name=f"xs{i}", align_bytes=64) for i in range(TILES)]
+        w_codes = [keep.tile([P, PASSES, 2 * CHUNK], U8, name=f"wc{c}", align_bytes=64) for c in range(CHUNKS)]
+        ws_first = keep.tile([P, PASSES, CHUNK], U8, align_bytes=64)
+        ws_rest = keep.tile([P, PASSES, (CHUNKS - 1) * CHUNK], U8, align_bytes=64)
+        cos_sb = keep.tile([P, 2, PAIR, HALF], BF16)
+        sin_sb = keep.tile([P, 2, PAIR, HALF], BF16)
+        g_sb = keep.tile([P, HD], BF16)
+        gain = keep.tile([P, HD], F32)
+        table = keep.tile([P, 2 * PAIR, 2, HD], F32)
+
+        def load_x(i):
+            for s in range(2):
+                nc.sync.dma_start(out=x_sb[i][s][:], in_=x_rows[i // PAIR, i % PAIR, :, s * D // 2 : (s + 1) * D // 2])
+
+        def load_scales(plane, first_col, last_col):
+            for q in range(4):
+                nc.sync.dma_start(
+                    out=plane[32 * q : 32 * q + 4, :, :].bitcast(I32),
+                    in_=Wq_scales[:, 4 * q : 4 * q + 4, first_col:last_col].rearrange("g r n -> r g n").bitcast(I32),
+                )
+
+        def load_w(c):
+            nc.sync.dma_start(
+                out=w_codes[c][:].bitcast(I32),
+                in_=Wq_words[:, :, 2 * CHUNK * c : 2 * CHUNK * (c + 1)].rearrange("g p n -> p g n").bitcast(I32),
+            )
+
+        def w_scale(c, g):
+            if c == 0:
+                return ws_first[:, g, :]
+            return ws_rest[:, g, (c - 1) * CHUNK : c * CHUNK]
+
+        xt_banks = {}
+        grouped = {}
+
+        def transpose_x(i):
+            for s in range(2):
+                words = x_sb[i][s][:].bitcast(F32)
+                xt = psum.tile([P, 2, 2, P], F32, tag="xt", bufs=2)
+                for g in range(2):
+                    for u in range(2):
+                        nc.tensor.transpose(xt[:, g, u, :], words[:, 256 * g + u : 256 * (g + 1) : 2], ident[:])
+                xt_banks[i, s] = xt
+
+        def copy_x(i):
+            grouped[i] = work.tile([P, PASSES * P * 4], BF16, name="grouped", bufs=2, align_bytes=64)
+            for s in range(2):
+                half = grouped[i][:, s * D // 2 : (s + 1) * D // 2].bitcast(F32)
+                nc.scalar.copy(
+                    out=half.rearrange("p (g r u) -> p g r u", g=2, u=2),
+                    in_=xt_banks[i, s][:].rearrange("p g u r -> p g r u"),
+                )
+
+        def quantize_x(i):
+            nc.vector.quantize_mx(out=x_codes[i][:].bitcast(E5M2X4), scales=x_scales[i][:], in_=grouped[i][:])
+
+        acc = {}
+        rstd = {}
+        prod = {}
+
+        def place(n):
+            group, rest = divmod(n, CHUNKS * PAIR)
+            c, j = divmod(rest, PAIR)
+            return group, c, j
+
+        def project(n):
+            group, c, j = place(n)
+            i = group * PAIR + j
+            acc[n] = psum.tile([P, CHUNK], F32, name="acc", bufs=6)
+            for g in range(PASSES):
+                nc.tensor.matmul_mx(
+                    out=acc[n][:],
+                    lhsT=x_codes[i][:, g * P : (g + 1) * P].bitcast(E5M2X4),
+                    lhsT_scale=x_scales[i][:, g * P : (g + 1) * P],
+                    rhs=w_codes[c][:, g, :].bitcast(E2M1X4),
+                    rhs_scale=w_scale(c, g),
+                    start=(g == 0),
+                    stop=(g == PASSES - 1),
+                )
+
+        def norm_stats(n):
+            squares = work.tile([P, HEADS, HD], F32, name="squares", bufs=2)
+            ssq = work.tile([P, HEADS], F32, name="ssq", bufs=4)
+            for h in range(HEADS):
+                nc.scalar.activation(
+                    out=squares[:, h, :], in_=acc[n][:, h * HD : (h + 1) * HD], func=ACT.Square, accum_out=ssq[:, h : h + 1]
+                )
+            rstd[n] = work.tile([P, HEADS], F32, name="rstd", bufs=4)
+            nc.scalar.activation(out=rstd[n][:], in_=ssq[:], func=ACT.Abs_reciprocal_sqrt, bias=EPS, scale=1.0 / HD)
+
+        def products(n):
+            group, c, j = place(n)
+            if j == 0:
+                prod[n // PAIR] = work.tile([P, HEADS, PAIR, 2, HD], F32, name="prod", bufs=4)
+            for h in range(HEADS):
+                nc.vector.scalar_tensor_tensor(
+                    out=prod[n // PAIR][:, h, j, :, :],
+                    in0=acc[n][:, h * HD : (h + 1) * HD].unsqueeze(1).to_broadcast([P, 2, HD]),
+                    scalar=rstd[n][:, h : h + 1],
+                    in1=table[:, (group % 2) * PAIR + j, :, :],
+                    op0=ALU.mult,
+                    op1=ALU.mult,
+                )
+
+        def rotate_and_store(m, engine, first, last):
+            group, c, j = place(m * PAIR)
+            both = prod[m][:, first:last].rearrange("p h j s d -> p (h j) s d")
+            res = work.tile([P, (last - first) * PAIR, HD], F32, name="res", bufs=6)
+            engine.tensor_tensor(out=res[:, :, :HALF], in0=both[:, :, 0, :HALF], in1=both[:, :, 1, HALF:], op=ALU.subtract)
+            engine.tensor_tensor(out=res[:, :, HALF:], in0=both[:, :, 0, HALF:], in1=both[:, :, 1, :HALF], op=ALU.add)
+            nc.sync.dma_start(
+                out=out_rows[group // 2, group % 2, :, c * HEADS + first : c * HEADS + last, :],
+                in_=res[:].rearrange("p (h j) d -> p h (j d)", j=PAIR),
+            )
+
+        make_identity(nc, ident[:])
+        nc.vector.memset(ws_first[:].bitcast(I32), 0)
+        nc.vector.memset(ws_rest[:].bitcast(I32), 0)
+        load_x(0)
+        load_x(1)
+        load_scales(ws_first, 0, CHUNK)
+        load_w(0)
+        nc.sync.dma_start(out=g_sb[:], in_=q_scale.partition_broadcast(P))
+        nc.sync.dma_start(out=cos_sb[:], in_=cos.rearrange("(u p j) d -> p u j d", p=P, j=PAIR))
+        nc.sync.dma_start(out=sin_sb[:], in_=sin.rearrange("(u p j) d -> p u j d", p=P, j=PAIR))
+        load_scales(ws_rest, CHUNK, CHUNKS * CHUNK)
+        load_w(1)
+        load_w(2)
+        load_x(2)
+        load_w(3)
+        load_x(3)
+
+        for i in range(PAIR):
+            transpose_x(i)
+            copy_x(i)
+            quantize_x(i)
+
+        nc.vector.tensor_scalar(out=gain[:], in0=g_sb[:], scalar1=1.0, scalar2=None, op0=ALU.add)
+        for s, trig in enumerate((cos_sb, sin_sb)):
+            nc.vector.tensor_tensor(
+                out=table[:, :, s, :].rearrange("p a (e d) -> p a e d", e=2),
+                in0=trig[:].rearrange("p u j d -> p (u j) d").unsqueeze(2).to_broadcast([P, 2 * PAIR, 2, HALF]),
+                in1=gain[:].rearrange("p (e d) -> p e d", e=2).unsqueeze(1).to_broadcast([P, 2 * PAIR, 2, HALF]),
+                op=ALU.mult,
+            )
+
+        for n in range(BANKS):
+            group, c, j = place(n)
+            ahead = (group + 1) * PAIR + c - 1
+            prepare = j == PAIR - 1 and c in (1, 2) and ahead < TILES
+            project(n)
+            if prepare:
+                transpose_x(ahead)
+            norm_stats(n)
+            if prepare:
+                copy_x(ahead)
+            products(n)
+            if prepare:
+                quantize_x(ahead)
+            if j == PAIR - 1:
+                if n // PAIR < BANKS // PAIR - VECTOR_PAIRS:
+                    rotate_and_store(n // PAIR, nc.gpsimd, 0, HEADS)
+                later = (group + 2) * PAIR + c
+                if c < PAIR and later < TILES:
+                    load_x(later)
+
+        for m in range(BANKS // PAIR - VECTOR_PAIRS, BANKS // PAIR):
+            rotate_and_store(m, nc.vector, 0, HEADS // 2)
+            rotate_and_store(m, nc.vector, HEADS // 2, HEADS)

@@ -29,6 +29,7 @@ GROUPS = B * T // GROUP
 TILES = GROUPS * PAIR
 BANKS = TILES * CHUNKS
 VECTOR_PAIRS = 2
+SCALE_RUNS = ((0, 1), (1, 4))
 
 
 def tile_multiheadattention_pa_kernel(tc, q_input, Wq_words, Wq_scales, q_scale, cos, sin, out):
@@ -43,27 +44,31 @@ def tile_multiheadattention_pa_kernel(tc, q_input, Wq_words, Wq_scales, q_scale,
         ctx.enter_context(tc.manual_schedule())
 
         ident = keep.tile([P, P], F32)
-        x_sb = [[keep.tile([P, D // 2], BF16, name=f"x{i}_{s}") for s in range(2)] for i in range(TILES)]
-        x_codes = [keep.tile([P, PASSES * P], U32, name=f"xc{i}", align_bytes=64) for i in range(TILES)]
-        x_scales = [keep.tile([P, PASSES * P], U8, name=f"xs{i}", align_bytes=64) for i in range(TILES)]
+        x_sb = [keep.tile([P, D], BF16, name=f"x{i}") for i in range(TILES)]
+        x_codes = [keep.tile([P, PAIR, PASSES * P], U32, name=f"xc{i}", align_bytes=64) for i in range(GROUPS)]
+        x_scales = [keep.tile([P, PAIR, PASSES * P], U8, name=f"xs{i}", align_bytes=64) for i in range(GROUPS)]
         w_codes = [keep.tile([P, PASSES, 2 * CHUNK], U8, name=f"wc{c}", align_bytes=64) for c in range(CHUNKS)]
-        ws_first = keep.tile([P, PASSES, CHUNK], U8, align_bytes=64)
-        ws_rest = keep.tile([P, PASSES, (CHUNKS - 1) * CHUNK], U8, align_bytes=64)
+        planes = [
+            keep.tile([P, PASSES, (last - first) * CHUNK], U8, name=f"ws{first}", align_bytes=64) for first, last in SCALE_RUNS
+        ]
+        ones = keep.tile([P, P], BF16)
         cos_sb = keep.tile([P, 2, PAIR, HALF], BF16)
         sin_sb = keep.tile([P, 2, PAIR, HALF], BF16)
         g_sb = keep.tile([P, HD], BF16)
         gain = keep.tile([P, HD], F32)
         table = keep.tile([P, 2 * PAIR, 2, HD], F32)
 
-        def load_x(i):
-            for s in range(2):
-                nc.sync.dma_start(out=x_sb[i][s][:], in_=x_rows[i // PAIR, i % PAIR, :, s * D // 2 : (s + 1) * D // 2])
+        def load_x(i, pieces=1):
+            for s in range(pieces):
+                cols = slice(s * D // pieces, (s + 1) * D // pieces)
+                nc.sync.dma_start(out=x_sb[i][:, cols], in_=x_rows[i // PAIR, i % PAIR, :, cols])
 
-        def load_scales(plane, first_col, last_col):
-            for q in range(4):
+        def load_scales(run):
+            first, last = SCALE_RUNS[run]
+            for r in range(4):
                 nc.sync.dma_start(
-                    out=plane[32 * q : 32 * q + 4, :, :].bitcast(I32),
-                    in_=Wq_scales[:, 4 * q : 4 * q + 4, first_col:last_col].rearrange("g r n -> r g n").bitcast(I32),
+                    out=planes[run][r:P:32, :, :].bitcast(I32),
+                    in_=Wq_scales[:, r:16:4, first * CHUNK : last * CHUNK].rearrange("g q n -> q g n").bitcast(I32),
                 )
 
         def load_w(c):
@@ -73,16 +78,16 @@ def tile_multiheadattention_pa_kernel(tc, q_input, Wq_words, Wq_scales, q_scale,
             )
 
         def w_scale(c, g):
-            if c == 0:
-                return ws_first[:, g, :]
-            return ws_rest[:, g, (c - 1) * CHUNK : c * CHUNK]
+            run = max(k for k, (first, last) in enumerate(SCALE_RUNS) if first <= c)
+            at = (c - SCALE_RUNS[run][0]) * CHUNK
+            return planes[run][:, g, at : at + CHUNK]
 
         xt_banks = {}
         grouped = {}
 
         def transpose_x(i):
             for s in range(2):
-                words = x_sb[i][s][:].bitcast(F32)
+                words = x_sb[i][:, s * D // 2 : (s + 1) * D // 2].bitcast(F32)
                 xt = psum.tile([P, 2, 2, P], F32, tag="xt", bufs=2)
                 for g in range(2):
                     for u in range(2):
@@ -90,16 +95,22 @@ def tile_multiheadattention_pa_kernel(tc, q_input, Wq_words, Wq_scales, q_scale,
                 xt_banks[i, s] = xt
 
         def copy_x(i):
-            grouped[i] = work.tile([P, PASSES * P * 4], BF16, name="grouped", bufs=2, align_bytes=64)
+            group, j = divmod(i, PAIR)
+            if j == 0:
+                grouped[group] = work.tile([P, PAIR, D], BF16, name="grouped", bufs=2, align_bytes=64)
             for s in range(2):
-                half = grouped[i][:, s * D // 2 : (s + 1) * D // 2].bitcast(F32)
+                half = grouped[group][:, j, s * D // 2 : (s + 1) * D // 2].bitcast(F32)
                 nc.scalar.copy(
                     out=half.rearrange("p (g r u) -> p g r u", g=2, u=2),
                     in_=xt_banks[i, s][:].rearrange("p g u r -> p g r u"),
                 )
 
-        def quantize_x(i):
-            nc.vector.quantize_mx(out=x_codes[i][:].bitcast(E5M2X4), scales=x_scales[i][:], in_=grouped[i][:])
+        def quantize_x(group, first, last):
+            nc.vector.quantize_mx(
+                out=x_codes[group][:, first:last, :].rearrange("p j c -> p (j c)").bitcast(E5M2X4),
+                scales=x_scales[group][:, first:last, :].rearrange("p j c -> p (j c)"),
+                in_=grouped[group][:, first:last, :].rearrange("p j c -> p (j c)"),
+            )
 
         acc = {}
         rstd = {}
@@ -112,13 +123,12 @@ def tile_multiheadattention_pa_kernel(tc, q_input, Wq_words, Wq_scales, q_scale,
 
         def project(n):
             group, c, j = place(n)
-            i = group * PAIR + j
             acc[n] = psum.tile([P, CHUNK], F32, name="acc", bufs=6)
             for g in range(PASSES):
                 nc.tensor.matmul_mx(
                     out=acc[n][:],
-                    lhsT=x_codes[i][:, g * P : (g + 1) * P].bitcast(E5M2X4),
-                    lhsT_scale=x_scales[i][:, g * P : (g + 1) * P],
+                    lhsT=x_codes[group][:, j, g * P : (g + 1) * P].bitcast(E5M2X4),
+                    lhsT_scale=x_scales[group][:, j, g * P : (g + 1) * P],
                     rhs=w_codes[c][:, g, :].bitcast(E2M1X4),
                     rhs_scale=w_scale(c, g),
                     start=(g == 0),
@@ -142,9 +152,9 @@ def tile_multiheadattention_pa_kernel(tc, q_input, Wq_words, Wq_scales, q_scale,
             for h in range(HEADS):
                 nc.vector.scalar_tensor_tensor(
                     out=prod[n // PAIR][:, h, j, :, :],
-                    in0=acc[n][:, h * HD : (h + 1) * HD].unsqueeze(1).to_broadcast([P, 2, HD]),
+                    in0=table[:, (group % 2) * PAIR + j, :, :],
                     scalar=rstd[n][:, h : h + 1],
-                    in1=table[:, (group % 2) * PAIR + j, :, :],
+                    in1=acc[n][:, h * HD : (h + 1) * HD].unsqueeze(1).to_broadcast([P, 2, HD]),
                     op0=ALU.mult,
                     op1=ALU.mult,
                 )
@@ -160,29 +170,33 @@ def tile_multiheadattention_pa_kernel(tc, q_input, Wq_words, Wq_scales, q_scale,
                 in_=res[:].rearrange("p (h j) d -> p h (j d)", j=PAIR),
             )
 
+        nc.gpsimd.memset(g_sb[:], 0.0)
         make_identity(nc, ident[:])
-        nc.vector.memset(ws_first[:].bitcast(I32), 0)
-        nc.vector.memset(ws_rest[:].bitcast(I32), 0)
-        load_x(0)
+        nc.gpsimd.memset(ones[:], 1.0)
+        for plane in planes:
+            nc.vector.memset(plane[:].bitcast(I32), 0)
+        load_x(0, pieces=2)
         load_x(1)
-        load_scales(ws_first, 0, CHUNK)
+        nc.sync.dma_start(out=g_sb[0:1, :], in_=q_scale.unsqueeze(0))
+        load_scales(0)
         load_w(0)
-        nc.sync.dma_start(out=g_sb[:], in_=q_scale.partition_broadcast(P))
         nc.sync.dma_start(out=cos_sb[:], in_=cos.rearrange("(u p j) d -> p u j d", p=P, j=PAIR))
         nc.sync.dma_start(out=sin_sb[:], in_=sin.rearrange("(u p j) d -> p u j d", p=P, j=PAIR))
-        load_scales(ws_rest, CHUNK, CHUNKS * CHUNK)
+        load_scales(1)
         load_w(1)
-        load_w(2)
         load_x(2)
-        load_w(3)
+        load_w(2)
         load_x(3)
+        load_w(3)
 
         for i in range(PAIR):
             transpose_x(i)
             copy_x(i)
-            quantize_x(i)
+            quantize_x(0, i, i + 1)
 
-        nc.vector.tensor_scalar(out=gain[:], in0=g_sb[:], scalar1=1.0, scalar2=None, op0=ALU.add)
+        g_all = psum.tile([P, HD], F32, name="acc", bufs=6)
+        nc.tensor.matmul(g_all[:], lhsT=ones[:], rhs=g_sb[:], start=True, stop=True)
+        nc.vector.tensor_scalar(out=gain[:], in0=g_all[:], scalar1=1.0, scalar2=None, op0=ALU.add)
         for s, trig in enumerate((cos_sb, sin_sb)):
             nc.vector.tensor_tensor(
                 out=table[:, :, s, :].rearrange("p a (e d) -> p a e d", e=2),
@@ -194,7 +208,7 @@ def tile_multiheadattention_pa_kernel(tc, q_input, Wq_words, Wq_scales, q_scale,
         for n in range(BANKS):
             group, c, j = place(n)
             ahead = (group + 1) * PAIR + c - 1
-            prepare = j == PAIR - 1 and c in (1, 2) and ahead < TILES
+            prepare = j == 0 and c in (1, 2) and ahead < TILES
             project(n)
             if prepare:
                 transpose_x(ahead)
@@ -202,8 +216,8 @@ def tile_multiheadattention_pa_kernel(tc, q_input, Wq_words, Wq_scales, q_scale,
             if prepare:
                 copy_x(ahead)
             products(n)
-            if prepare:
-                quantize_x(ahead)
+            if c == PAIR and j == 0 and group + 1 < GROUPS:
+                quantize_x(group + 1, 0, PAIR)
             if j == PAIR - 1:
                 if n // PAIR < BANKS // PAIR - VECTOR_PAIRS:
                     rotate_and_store(n // PAIR, nc.gpsimd, 0, HEADS)

from contextlib import ExitStack

import concourse.mybir as mybir
from concourse.masks import make_identity

B, T, D, H, HD = 2, 512, 2048, 16, 128
HALF = HD // 2
EPS = 1e-6
FLOPS = 2 * B * T * D * H * HD

F32 = mybir.dt.float32
BF16 = mybir.dt.bfloat16
I32 = mybir.dt.int32
U32 = mybir.dt.uint32
U8 = mybir.dt.uint8
E5M2X4 = mybir.dt.float8_e5m2_x4
E2M1X4 = mybir.dt.float4_e2m1fn_x4
ALU = mybir.AluOpType
ACT = mybir.ActivationFunctionType

P = 128
PASSES = D // 512
CHUNK = 512
CHUNKS = H * HD // CHUNK
HEADS = CHUNK // HD
PAIR = 2
GROUP = P * PAIR
GROUPS = B * T // GROUP
TILES = GROUPS * PAIR
BANKS = TILES * CHUNKS
VECTOR_PAIRS = 2
SCALE_RUNS = ((0, 1), (1, 4))


def tile_multiheadattention_pa_kernel(tc, q_input, Wq_words, Wq_scales, q_scale, cos, sin, out):
    nc = tc.nc
    x_rows = q_input.rearrange("b (u p j) k -> (b u) j p k", p=P, j=PAIR)
    out_rows = out.rearrange("b h (u p j) d -> b u p h (j d)", p=P, j=PAIR)

    with ExitStack() as ctx:
        keep = ctx.enter_context(tc.tile_pool(name="keep", bufs=1))
        work = ctx.enter_context(tc.tile_pool(name="work", bufs=2))
        psum = ctx.enter_context(tc.psum_pool(name="psum", bufs=2))
        ctx.enter_context(tc.manual_schedule())

        ident = keep.tile([P, P], F32)
        x_sb = [keep.tile([P, D], BF16, name=f"x{i}") for i in range(TILES)]
        x_codes = [keep.tile([P, PAIR, PASSES * P], U32, name=f"xc{i}", align_bytes=64) for i in range(GROUPS)]
        x_scales = [keep.tile([P, PAIR, PASSES * P], U8, name=f"xs{i}", align_bytes=64) for i in range(GROUPS)]
        w_codes = [keep.tile([P, PASSES, 2 * CHUNK], U8, name=f"wc{c}", align_bytes=64) for c in range(CHUNKS)]
        planes = [
            keep.tile([P, PASSES, (last - first) * CHUNK], U8, name=f"ws{first}", align_bytes=64) for first, last in SCALE_RUNS
        ]
        ones = keep.tile([P, P], BF16)
        cos_sb = keep.tile([P, 2, PAIR, HALF], BF16)
        sin_sb = keep.tile([P, 2, PAIR, HALF], BF16)
        g_sb = keep.tile([P, HD], BF16)
        gain = keep.tile([P, HD], F32)
        table = keep.tile([P, 2 * PAIR, 2, HD], F32)

        def load_x(i, pieces=1):
            for s in range(pieces):
                cols = slice(s * D // pieces, (s + 1) * D // pieces)
                nc.sync.dma_start(out=x_sb[i][:, cols], in_=x_rows[i // PAIR, i % PAIR, :, cols])

        def load_scales(run):
            first, last = SCALE_RUNS[run]
            for r in range(4):
                nc.sync.dma_start(
                    out=planes[run][r:P:32, :, :].bitcast(I32),
                    in_=Wq_scales[:, r:16:4, first * CHUNK : last * CHUNK].rearrange("g q n -> q g n").bitcast(I32),
                )

        def load_w(c):
            nc.sync.dma_start(
                out=w_codes[c][:].bitcast(I32),
                in_=Wq_words[:, :, 2 * CHUNK * c : 2 * CHUNK * (c + 1)].rearrange("g p n -> p g n").bitcast(I32),
            )

        def w_scale(c, g):
            run = max(k for k, (first, last) in enumerate(SCALE_RUNS) if first <= c)
            at = (c - SCALE_RUNS[run][0]) * CHUNK
            return planes[run][:, g, at : at + CHUNK]

        xt_banks = {}
        grouped = {}

        def transpose_x(i):
            for s in range(2):
                words = x_sb[i][:, s * D // 2 : (s + 1) * D // 2].bitcast(F32)
                xt = psum.tile([P, 2, 2, P], F32, tag="xt", bufs=2)
                for g in range(2):
                    for u in range(2):
                        nc.tensor.transpose(xt[:, g, u, :], words[:, 256 * g + u : 256 * (g + 1) : 2], ident[:])
                xt_banks[i, s] = xt

        def copy_x(i):
            group, j = divmod(i, PAIR)
            if j == 0:
                grouped[group] = work.tile([P, PAIR, D], BF16, name="grouped", bufs=2, align_bytes=64)
            for s in range(2):
                half = grouped[group][:, j, s * D // 2 : (s + 1) * D // 2].bitcast(F32)
                nc.scalar.copy(
                    out=half.rearrange("p (g r u) -> p g r u", g=2, u=2),
                    in_=xt_banks[i, s][:].rearrange("p g u r -> p g r u"),
                )

        def quantize_x(group, first, last):
            nc.vector.quantize_mx(
                out=x_codes[group][:, first:last, :].rearrange("p j c -> p (j c)").bitcast(E5M2X4),
                scales=x_scales[group][:, first:last, :].rearrange("p j c -> p (j c)"),
                in_=grouped[group][:, first:last, :].rearrange("p j c -> p (j c)"),
            )

        acc = {}
        rstd = {}
        prod = {}

        def place(n):
            group, rest = divmod(n, CHUNKS * PAIR)
            c, j = divmod(rest, PAIR)
            return group, c, j

        def project(n):
            group, c, j = place(n)
            acc[n] = psum.tile([P, CHUNK], F32, name="acc", bufs=6)
            for g in range(PASSES):
                nc.tensor.matmul_mx(
                    out=acc[n][:],
                    lhsT=x_codes[group][:, j, g * P : (g + 1) * P].bitcast(E5M2X4),
                    lhsT_scale=x_scales[group][:, j, g * P : (g + 1) * P],
                    rhs=w_codes[c][:, g, :].bitcast(E2M1X4),
                    rhs_scale=w_scale(c, g),
                    start=(g == 0),
                    stop=(g == PASSES - 1),
                )

        def norm_stats(n):
            squares = work.tile([P, HEADS, HD], F32, name="squares", bufs=2)
            ssq = work.tile([P, HEADS], F32, name="ssq", bufs=4)
            for h in range(HEADS):
                nc.scalar.activation(
                    out=squares[:, h, :], in_=acc[n][:, h * HD : (h + 1) * HD], func=ACT.Square, accum_out=ssq[:, h : h + 1]
                )
            rstd[n] = work.tile([P, HEADS], F32, name="rstd", bufs=4)
            nc.scalar.activation(out=rstd[n][:], in_=ssq[:], func=ACT.Abs_reciprocal_sqrt, bias=EPS, scale=1.0 / HD)

        def products(n):
            group, c, j = place(n)
            if j == 0:
                prod[n // PAIR] = work.tile([P, HEADS, PAIR, 2, HD], F32, name="prod", bufs=4)
            for h in range(HEADS):
                nc.vector.scalar_tensor_tensor(
                    out=prod[n // PAIR][:, h, j, :, :],
                    in0=table[:, (group % 2) * PAIR + j, :, :],
                    scalar=rstd[n][:, h : h + 1],
                    in1=acc[n][:, h * HD : (h + 1) * HD].unsqueeze(1).to_broadcast([P, 2, HD]),
                    op0=ALU.mult,
                    op1=ALU.mult,
                )

        def rotate_and_store(m, engine, first, last):
            group, c, j = place(m * PAIR)
            both = prod[m][:, first:last].rearrange("p h j s d -> p (h j) s d")
            res = work.tile([P, (last - first) * PAIR, HD], F32, name="res", bufs=6)
            engine.tensor_tensor(out=res[:, :, :HALF], in0=both[:, :, 0, :HALF], in1=both[:, :, 1, HALF:], op=ALU.subtract)
            engine.tensor_tensor(out=res[:, :, HALF:], in0=both[:, :, 0, HALF:], in1=both[:, :, 1, :HALF], op=ALU.add)
            nc.sync.dma_start(
                out=out_rows[group // 2, group % 2, :, c * HEADS + first : c * HEADS + last, :],
                in_=res[:].rearrange("p (h j) d -> p h (j d)", j=PAIR),
            )

        nc.gpsimd.memset(g_sb[:], 0.0)
        make_identity(nc, ident[:])
        nc.gpsimd.memset(ones[:], 1.0)
        for plane in planes:
            nc.vector.memset(plane[:].bitcast(I32), 0)
        load_x(0, pieces=2)
        load_x(1)
        nc.sync.dma_start(out=g_sb[0:1, :], in_=q_scale.unsqueeze(0))
        load_scales(0)
        load_w(0)
        nc.sync.dma_start(out=cos_sb[:], in_=cos.rearrange("(u p j) d -> p u j d", p=P, j=PAIR))
        nc.sync.dma_start(out=sin_sb[:], in_=sin.rearrange("(u p j) d -> p u j d", p=P, j=PAIR))
        load_scales(1)
        load_w(1)
        load_x(2)
        load_w(2)
        load_x(3)
        load_w(3)

        for i in range(PAIR):
            transpose_x(i)
            copy_x(i)
            quantize_x(0, i, i + 1)

        g_all = psum.tile([P, HD], F32, name="acc", bufs=6)
        nc.tensor.matmul(g_all[:], lhsT=ones[:], rhs=g_sb[:], start=True, stop=True)
        nc.vector.tensor_scalar(out=gain[:], in0=g_all[:], scalar1=1.0, scalar2=None, op0=ALU.add)
        for s, trig in enumerate((cos_sb, sin_sb)):
            nc.vector.tensor_tensor(
                out=table[:, :, s, :].rearrange("p a (e d) -> p a e d", e=2),
                in0=trig[:].rearrange("p u j d -> p (u j) d").unsqueeze(2).to_broadcast([P, 2 * PAIR, 2, HALF]),
                in1=gain[:].rearrange("p (e d) -> p e d", e=2).unsqueeze(1).to_broadcast([P, 2 * PAIR, 2, HALF]),
                op=ALU.mult,
            )

        for n in range(BANKS):
            group, c, j = place(n)
            ahead = (group + 1) * PAIR + c - 1
            prepare = j == 0 and c in (1, 2) and ahead < TILES
            project(n)
            if prepare:
                transpose_x(ahead)
            norm_stats(n)
            if prepare:
                copy_x(ahead)
            products(n)
            if c == PAIR and j == 0 and group + 1 < GROUPS:
                quantize_x(group + 1, 0, PAIR)
            if j == PAIR - 1:
                if n // PAIR < BANKS // PAIR - VECTOR_PAIRS:
                    rotate_and_store(n // PAIR, nc.gpsimd, 0, HEADS)
                later = (group + 2) * PAIR + c
                if c < PAIR and later < TILES:
                    load_x(later)

        for m in range(BANKS // PAIR - VECTOR_PAIRS, BANKS // PAIR):
            rotate_and_store(m, nc.vector, 0, HEADS // 2)
            rotate_and_store(m, nc.vector, HEADS // 2, HEADS)
